import numpy as np
import ml_dtypes


def mxq(x, axis, fmt="e4m3"):
    dtype, down = {"e4m3": (ml_dtypes.float8_e4m3fn, 7), "e5m2": (ml_dtypes.float8_e5m2, 14)}[fmt]
    v = np.moveaxis(np.asarray(x, np.float32).astype(ml_dtypes.bfloat16).astype(np.float64), axis, -1)
    blocks = v.reshape(v.shape[:-1] + (-1, 32))
    amax = np.abs(blocks).max(-1, keepdims=True)
    byte = np.maximum(np.where(amax > 0, np.frexp(amax)[1] - 1 + 127, 0) - down, 1)
    scale = np.exp2(byte - 127.0)
    codes = (blocks / scale).astype(np.float32).astype(dtype).astype(np.float64)
    return np.moveaxis((codes * scale).reshape(v.shape), -1, axis)


WIDE = False


def mx_kscale(k):
    if not WIDE:
        return np.ones(k)
    levels = np.array([10, -10, 5, -5, 0])
    if k % 512:
        return np.exp2(np.random.permutation(np.resize(levels, k // 32))).repeat(32)
    a = np.empty((k // 512, 16))
    for p in range(k // 512):
        a[p, :8] = np.random.permutation(np.resize(levels, 8))
        for g in range(8):
            far = levels[np.abs(levels - a[p, g]) >= 10]
            a[p, g + 8] = far[np.random.randint(len(far))]
    return np.exp2(a.ravel()).repeat(32)


BF16 = ml_dtypes.bfloat16


def bf(x):
    return np.asarray(x, np.float32).astype(BF16)


def f64(x):
    return np.asarray(x).astype(np.float64)


B, N, D, LAYER_NUM = 16, 128, 512, 2


def draw0():
    fin = mx_kscale(D)
    user = bf(np.random.standard_normal((B, N, D)) * fin)
    parts = []
    for l in range(LAYER_NUM):
        fout = mx_kscale(D) if l + 1 < LAYER_NUM else np.ones(D)
        parts.append((np.random.standard_normal((B, D, D)) * 1.2 / np.sqrt(D) / fin[:, None] * fout).reshape(B, D * D))
        parts.append(np.random.standard_normal((B, D)) * 0.5 * fout)
        fin = fout
    return {"user_emb": user, "item_emb": bf(np.concatenate(parts, axis=1))}


def core(user_emb, item_emb):
    x = f64(user_emb)
    item = f64(item_emb)
    nb = x.shape[0]
    off = 0
    for _ in range(LAYER_NUM):
        W = item[:, off:off + D * D].reshape(nb, D, D)
        off += D * D
        b = item[:, off:off + D].reshape(nb, 1, D)
        off += D
        x = np.maximum((mxq(x, 2, "e4m3") @ mxq(W, 1, "e4m3")) + b, 0.0)
    return x


def e4m3fn_bytes(y):
    return np.clip(np.asarray(y, np.float64), -448.0, 448.0).astype(np.float32).astype(ml_dtypes.float8_e4m3fn).view(np.uint8)


def e4m3fn_values(b):
    return np.asarray(b, np.uint8).view(ml_dtypes.float8_e4m3fn).astype(np.float64)


def setup_inputs():
    d = draw0()
    x0 = np.asarray(d['user_emb']).astype(np.float64)
    s = (np.max(np.abs(x0), axis=(0, 1), keepdims=True) / 448.0).astype(np.float32)
    out = {}
    for k, v in d.items():
        if k == 'user_emb':
            out['user_emb_bytes'] = e4m3fn_bytes(x0 / s.astype(np.float64))
            out['user_emb_scale'] = s
        else:
            out[k] = v
    return out


def reference(user_emb_bytes, user_emb_scale, item_emb):
    return core(e4m3fn_values(user_emb_bytes) * user_emb_scale.astype(np.float64), item_emb)

@@ -1,0 +1,301 @@
+from contextlib import ExitStack
+
+import concourse.mybir as mybir
+from concourse.masks import make_identity
+
+P = 128
+NB, D = 16, 512
+W_LEN = D * D
+SAMPLE = 2 * (W_LEN + D)
+PACK = 4
+
+F32 = mybir.dt.float32
+BF16 = mybir.dt.bfloat16
+U32 = mybir.dt.uint32
+U8 = mybir.dt.uint8
+FP8 = mybir.dt.float8_e4m3fn
+FP8X4 = mybir.dt.float8_e4m3fn_x4
+ACT = mybir.ActivationFunctionType
+ALU = mybir.AluOpType
+
+FLOPS = 2 * 2 * NB * P * D * D
+
+S_M = 32
+S_C = 128
+AHEAD = 6
+RUN = 4
+
+
+def tile_can_kernel(tc, xbytes, xscale, item, out):
+    nc = tc.nc
+    with ExitStack() as ctx:
+        const = ctx.enter_context(tc.tile_pool(name="const", bufs=1))
+        rawp = ctx.enter_context(tc.tile_pool(name="rawp", bufs=AHEAD))
+        work = ctx.enter_context(tc.tile_pool(name="work", bufs=3))
+        psum = ctx.enter_context(tc.psum_pool(name="psum", bufs=2))
+        ctx.enter_context(tc.manual_schedule())
+
+        raw0, raw1 = {}, {}
+        g0, g1 = {}, {}
+        c0, s0, c1, s1 = {}, {}, {}, {}
+        xs, xt, xg, xc, xsc = {}, {}, {}, {}, {}
+        z1, hp, hg, hc, hsc = {}, {}, {}, {}, {}
+        z2, y, o, res = {}, {}, {}, {}
+
+        s4 = const.tile([P, PACK], F32, name="s4")
+        brow = const.tile([P, 2, D], BF16, name="brow")
+        dummy = const.tile([P, 1], F32, name="dummy")
+        ident = const.tile([P, P], F32, name="ident")
+        ident_bf = const.tile([P, P], BF16, name="ident_bf")
+        scale_all = const.tile([P, P, PACK], F32, name="scale_all")
+        bias = const.tile([P, 8, NB], F32, name="bias")
+        x_bytes = const.tile([P, NB, D], U8, name="x_bytes")
+
+        nc.scalar.dma_start(out=s4[:], in_=xscale.rearrange("a q (p j) -> p (a q j)", j=PACK))
+        nc.vector.memset(dummy[:], 0.0)
+        nc.vector.memset(brow[:], 0.0)
+        nc.scalar.dma_start(out=brow[0:NB, 0, :], in_=item[:, W_LEN:W_LEN + D])
+        nc.scalar.dma_start(out=brow[0:NB, 1, :], in_=item[:, SAMPLE - D:SAMPLE])
+        nc.scalar.activation(out=dummy[:], in_=dummy[:], func=ACT.Relu)
+        make_identity(nc, ident[:])
+        nc.vector.tensor_copy(out=ident_bf[:], in_=ident[:])
+
+        def load_x(b0, b1):
+            nc.sync.dma_start(out=x_bytes[:, b0:b1, :], in_=xbytes[b0:b1].rearrange("b r k -> r b k"))
+
+        def w_src(b, layer):
+            off = layer * (W_LEN + D)
+            return item[b, off:off + W_LEN].rearrange("(p j c) -> p j c", j=PACK, c=D)
+
+        def load_w0(b, pieces):
+            r = rawp.tile([P, PACK, D], BF16, name="raw0", tag="raw0", align_bytes=64)
+            raw0[b] = r
+            step = D // pieces
+            for q in range(pieces):
+                nc.sync.dma_start(out=r[:, :, q * step:(q + 1) * step], in_=w_src(b, 0)[:, :, q * step:(q + 1) * step])
+
+        def load_w1(b):
+            r = rawp.tile([P, PACK, D], BF16, name="raw1", tag="raw1", align_bytes=64)
+            raw1[b] = r
+            nc.sync.dma_start(out=r[:], in_=w_src(b, 1))
+
+        def xprod(b):
+            t = work.tile([P, D], BF16, name="xs", tag="xs", align_bytes=64)
+            xs[b] = t
+            nc.vector.tensor_tensor(out=t[:], in0=x_bytes[:, b, :].bitcast(FP8),
+                                    in1=scale_all[:].rearrange("p n j -> p (n j)"), op=ALU.mult)
+
+        def xtrans(b):
+            t = psum.tile([P, 2, P], F32, name="xt", tag="xt")
+            xt[b] = t
+            words = xs[b][:].bitcast(F32)
+            for u in range(2):
+                nc.tensor.transpose(t[:, u, :], words[:, u:D // 2:2], ident[:])
+
+        def xcopy(b):
+            t = work.tile([P, P, PACK], BF16, name="xg", tag="xg", align_bytes=64)
+            xg[b] = t
+            nc.scalar.copy(out=t[:].rearrange("p r j -> p (r j)").bitcast(F32).rearrange("p (r u) -> p r u", u=2),
+                           in_=xt[b][:].rearrange("p u r -> p r u"))
+
+        def quant(src, width, kind, codes, scales, b):
+            c = work.tile([P, width], U32, name="c_" + kind, tag="c_" + kind, align_bytes=64)
+            s = work.tile([P, width], U8, name="s_" + kind, tag="s_" + kind, align_bytes=64)
+            codes[b], scales[b] = c, s
+            nc.vector.quantize_mx(out=c[:].bitcast(FP8X4), scales=s[:], in_=src)
+
+        def qx(b):
+            quant(xg[b][:].rearrange("p r j -> p (r j)"), P, "x", xc, xsc, b)
+
+        def q0(b):
+            quant(g0[b][:].rearrange("p t m j -> p (t m j)"), D, "w0", c0, s0, b)
+
+        def q1(b):
+            quant(g1[b][:].rearrange("p c j -> p (c j)"), D, "w1", c1, s1, b)
+
+        def qh(b):
+            quant(hg[b][:].rearrange("p n j -> p (n j)"), P, "h", hc, hsc, b)
+
+        def new_g0(b):
+            g0[b] = work.tile([P, PACK, P, PACK], BF16, name="g0", tag="g0", align_bytes=64)
+
+        def new_g1(b):
+            g1[b] = work.tile([P, D, PACK], BF16, name="g1", tag="g1", align_bytes=64)
+
+        def ilv0(copy, b, m0, m1):
+            copy(out=g0[b][:, :, m0:m1, :].rearrange("p t m j -> p m j t"),
+                 in_=raw0[b][:, :, PACK * m0:PACK * m1].rearrange("p j (m t) -> p m j t", t=PACK))
+
+        def ilv1(copy, b, lo, hi):
+            copy(out=g1[b][:, lo:hi, :].rearrange("p (c i) j -> p c j i", i=RUN),
+                 in_=raw1[b][:, :, lo:hi].rearrange("p j (c i) -> p c j i", i=RUN))
+
+        def mm1(b):
+            t4 = psum.tile([P, PACK, P], F32, name="z1", tag="z1")
+            z1[b] = t4
+            for t in range(PACK):
+                nc.tensor.matmul_mx(out=t4[:, t, :], lhsT=c0[b][:, t * P:(t + 1) * P].bitcast(FP8X4),
+                                    lhsT_scale=s0[b][:, t * P:(t + 1) * P],
+                                    rhs=xc[b][:].bitcast(FP8X4), rhs_scale=xsc[b][:], start=True, stop=True)
+
+        def hact(b):
+            t4 = work.tile([P, PACK, P], BF16, name="hp", tag="hp", align_bytes=64)
+            hp[b] = t4
+            for t in range(PACK):
+                nc.scalar.activation(out=t4[:, t, :], in_=z1[b][:, t, :], func=ACT.Relu, bias=bias[:, t, b:b + 1])
+
+        def hilv(copy, b):
+            t4 = work.tile([P, P, PACK], BF16, name="hg", tag="hg", align_bytes=64)
+            hg[b] = t4
+            copy(out=t4[:].rearrange("p (c i) j -> p c j i", i=RUN),
+                 in_=hp[b][:].rearrange("p j (c i) -> p c j i", i=RUN))
+
+        def mm2_into(dst, b, T):
+            nc.tensor.matmul_mx(out=dst, lhsT=c1[b][:, T * P:(T + 1) * P].bitcast(FP8X4),
+                                lhsT_scale=s1[b][:, T * P:(T + 1) * P],
+                                rhs=hc[b][:].bitcast(FP8X4), rhs_scale=hsc[b][:], start=True, stop=True)
+
+        def mm2(b):
+            t4 = psum.tile([P, PACK, P], F32, name="z2", tag="z2")
+            z2[b] = t4
+            for T in range(PACK):
+                mm2_into(t4[:, T, :], b, T)
+
+        def yact(b):
+            t4 = work.tile([P, PACK, P], F32, name="y", tag="y", align_bytes=64)
+            y[b] = t4
+            for T in range(PACK):
+                nc.scalar.activation(out=t4[:, T, :], in_=z2[b][:, T, :], func=ACT.Relu, bias=bias[:, PACK + T, b:b + 1])
+
+        def otrans(b):
+            t4 = psum.tile([P, PACK, P], F32, name="o", tag="o")
+            o[b] = t4
+            for T in range(PACK):
+                nc.tensor.transpose(t4[:, T, :], y[b][:, T, :], ident[:])
+
+        def ocopy(b):
+            t = work.tile([P, D], F32, name="res", tag="res", align_bytes=64)
+            res[b] = t
+            nc.scalar.copy(out=t[:], in_=o[b][:].rearrange("p t n -> p (t n)"))
+
+        def store(b):
+            nc.sync.dma_start(out=out[b], in_=res[b][:])
+
+        load_x(0, 1)
+        load_w0(0, 2)
+        load_w1(0)
+        load_x(1, 4)
+        load_w0(1, 1)
+        load_w1(1)
+        load_x(4, NB)
+        for b in range(2, AHEAD):
+            load_w0(b, 1)
+            load_w1(b)
+
+        spread = psum.tile([P, PACK, P], F32, name="spread", tag="o")
+        for j in range(PACK):
+            nc.tensor.transpose(spread[:, j, :], s4[:, j:j + 1].to_broadcast([P, P]), ident[:])
+        nc.scalar.copy(out=scale_all[:], in_=spread[:].rearrange("p j n -> p n j"))
+
+        biases = psum.tile([P, 8, P], BF16, name="biases", tag="z2")
+        for t in range(PACK):
+            nc.tensor.transpose(biases[:, t, :], brow[:, 0, t:D:PACK], ident_bf[:])
+        for t in range(PACK):
+            nc.tensor.transpose(biases[:, PACK + t, :], brow[:, 1, t * P:(t + 1) * P], ident_bf[:])
+
+        V, S = nc.vector.tensor_copy, nc.scalar.copy
+        xprod(0)
+        xtrans(0)
+        new_g0(0)
+        ilv0(S, 0, 0, 20)
+        ilv0(V, 0, 20, 64)
+        xcopy(0)
+        ilv0(V, 0, 64, 108)
+        ilv0(S, 0, 108, 128)
+        qx(0)
+        xprod(1)
+        q0(0)
+        mm1(0)
+        xtrans(1)
+        nc.vector.tensor_copy(out=bias[:], in_=biases[:, :, 0:NB])
+        new_g1(0)
+        ilv1(S, 0, D - S_C, D)
+        ilv1(V, 0, 0, D - S_C)
+        xcopy(1)
+        hact(0)
+        qx(1)
+
+        for i in range(NB):
+            if i >= 1:
+                mm2(i - 1)
+            if i + 2 < NB:
+                xprod(i + 2)
+            if i + 1 < NB:
+                new_g0(i + 1)
+                ilv0(S, i + 1, P - S_M, P)
+                ilv0(V, i + 1, 0, P - S_M)
+            if i == NB - 1:
+                hilv(S, i)
+            if i >= 1:
+                yact(i - 1)
+            if i + 2 < NB:
+                xtrans(i + 2)
+            if i >= 1:
+                otrans(i - 1)
+            if i < NB - 1:
+                hilv(S, i)
+            if i + 2 < NB:
+                xcopy(i + 2)
+            q1(i)
+            if i + 1 < NB:
+                q0(i + 1)
+                mm1(i + 1)
+            if i >= 1:
+                ocopy(i - 1)
+            if i + AHEAD < NB:
+                load_w0(i + AHEAD, 1)
+            if i >= 1:
+                store(i - 1)
+            if i + AHEAD < NB:
+                load_w1(i + AHEAD)
+            if i + 1 < NB:
+                new_g1(i + 1)
+                ilv1(S, i + 1, D - S_C, D)
+                ilv1(V, i + 1, 0, D - S_C)
+                hact(i + 1)
+            qh(i)
+            if i + 2 < NB:
+                qx(i + 2)
+
+        b = NB - 1
+        halves = []
+        for h in range(2):
+            zh = psum.tile([P, 2, P], F32, name="zh", tag="z2")
+            for T in range(2):
+                mm2_into(zh[:, T, :], b, 2 * h + T)
+            halves.append(zh)
+        ys, os_ = [], []
+        for h in range(2):
+            yh = work.tile([P, 2, P], F32, name="yh", tag="y", align_bytes=64)
+            for T in range(2):
+                col = bias[:, PACK + 2 * h + T, b:b + 1]
+                if h == 0:
+                    nc.scalar.activation(out=yh[:, T, :], in_=halves[h][:, T, :], func=ACT.Relu, bias=col)
+                else:
+                    nc.vector.tensor_scalar(out=yh[:, T, :], in0=halves[h][:, T, :], scalar1=col, scalar2=0.0,
+                                            op0=ALU.add, op1=ALU.max)
+            ys.append(yh)
+        for h in range(2):
+            oh = psum.tile([P, 2, P], F32, name="oh", tag="o")
+            for T in range(2):
+                nc.tensor.transpose(oh[:, T, :], ys[h][:, T, :], ident[:])
+            os_.append(oh)
+        for h in range(2):
+            rh = work.tile([P, 2 * P], F32, name="rh", tag="res", align_bytes=64)
+            cols = slice(2 * P * h, 2 * P * (h + 1))
+            if h == 0:
+                nc.scalar.copy(out=rh[:], in_=os_[h][:].rearrange("p t n -> p (t n)"))
+                nc.sync.dma_start(out=out[b, :, cols], in_=rh[:])
+            else:
+                nc.vector.tensor_copy(out=rh[:], in_=os_[h][:].rearrange("p t n -> p (t n)"))
+                nc.scalar.dma_start(out=out[b, :, cols], in_=rh[:])

@@ -23,7 +23,7 @@ FLOPS = 2 * 2 * NB * P * D * D
 S_M = 32
 S_C = 128
 AHEAD = 6
-RUN = 4
+RUN = 8
 
 
 def tile_can_kernel(tc, xbytes, xscale, item, out):
@@ -123,8 +123,8 @@ def tile_can_kernel(tc, xbytes, xscale, item, out):
             g1[b] = work.tile([P, D, PACK], BF16, name="g1", tag="g1", align_bytes=64)
 
         def ilv0(copy, b, m0, m1):
-            copy(out=g0[b][:, :, m0:m1, :].rearrange("p t m j -> p m j t"),
-                 in_=raw0[b][:, :, PACK * m0:PACK * m1].rearrange("p j (m t) -> p m j t", t=PACK))
+            copy(out=g0[b][:, :, m0:m1, :].rearrange("p t (m e) j -> p m j t e", e=2),
+                 in_=raw0[b][:, :, PACK * m0:PACK * m1].rearrange("p j (m e t) -> p m j t e", e=2, t=PACK))
 
         def ilv1(copy, b, lo, hi):
             copy(out=g1[b][:, lo:hi, :].rearrange("p (c i) j -> p c j i", i=RUN),

@@ -20,8 +20,8 @@ ALU = mybir.AluOpType
 
 FLOPS = 2 * 2 * NB * P * D * D
 
-S_M = 32
-S_C = 128
+S_M = 28
+S_C = 112
 AHEAD = 6
 RUN = 8
 
@@ -144,11 +144,12 @@ def tile_can_kernel(tc, xbytes, xscale, item, out):
             for t in range(PACK):
                 nc.scalar.activation(out=t4[:, t, :], in_=z1[b][:, t, :], func=ACT.Relu, bias=bias[:, t, b:b + 1])
 
-        def hilv(copy, b):
-            t4 = work.tile([P, P, PACK], BF16, name="hg", tag="hg", align_bytes=64)
-            hg[b] = t4
-            copy(out=t4[:].rearrange("p (c i) j -> p c j i", i=RUN),
-                 in_=hp[b][:].rearrange("p j (c i) -> p c j i", i=RUN))
+        def new_hg(b):
+            hg[b] = work.tile([P, P, PACK], BF16, name="hg", tag="hg", align_bytes=64)
+
+        def hilv(copy, b, lo, hi):
+            copy(out=hg[b][:, lo:hi, :].rearrange("p (c i) j -> p c j i", i=RUN),
+                 in_=hp[b][:, :, lo:hi].rearrange("p j (c i) -> p c j i", i=RUN))
 
         def mm2_into(dst, b, T):
             nc.tensor.matmul_mx(out=dst, lhsT=c1[b][:, T * P:(T + 1) * P].bitcast(FP8X4),
@@ -173,10 +174,10 @@ def tile_can_kernel(tc, xbytes, xscale, item, out):
             for T in range(PACK):
                 nc.tensor.transpose(t4[:, T, :], y[b][:, T, :], ident[:])
 
-        def ocopy(b):
+        def ocopy(copy, b):
             t = work.tile([P, D], F32, name="res", tag="res", align_bytes=64)
             res[b] = t
-            nc.scalar.copy(out=t[:], in_=o[b][:].rearrange("p t n -> p (t n)"))
+            copy(out=t[:], in_=o[b][:].rearrange("p t n -> p (t n)"))
 
         def store(b):
             nc.sync.dma_start(out=out[b], in_=res[b][:])
@@ -214,66 +215,72 @@ def tile_can_kernel(tc, xbytes, xscale, item, out):
         ilv0(S, 0, 108, 128)
         qx(0)
         xprod(1)
+        xtrans(1)
         q0(0)
         mm1(0)
-        xtrans(1)
         nc.vector.tensor_copy(out=bias[:], in_=biases[:, :, 0:NB])
+        xcopy(1)
         new_g1(0)
         ilv1(S, 0, D - S_C, D)
         ilv1(V, 0, 0, D - S_C)
-        xcopy(1)
-        hact(0)
         qx(1)
 
-        for i in range(NB):
-            if i >= 1:
-                mm2(i - 1)
+        last = NB - 1
+        for i in range(last):
             if i + 2 < NB:
                 xprod(i + 2)
-            if i + 1 < NB:
-                new_g0(i + 1)
-                ilv0(S, i + 1, P - S_M, P)
-                ilv0(V, i + 1, 0, P - S_M)
-            if i == NB - 1:
-                hilv(S, i)
-            if i >= 1:
-                yact(i - 1)
+            new_g0(i + 1)
+            ilv0(S, i + 1, P - S_M, P)
+            ilv0(V, i + 1, 0, P - S_M)
             if i + 2 < NB:
                 xtrans(i + 2)
+            if i >= 2:
+                otrans(i - 2)
+            hact(i)
             if i >= 1:
-                otrans(i - 1)
-            if i < NB - 1:
-                hilv(S, i)
+                yact(i - 1)
+            new_hg(i)
+            hilv(S, i, 0, P)
+            q1(i)
+            q0(i + 1)
+            mm1(i + 1)
             if i + 2 < NB:
                 xcopy(i + 2)
-            q1(i)
-            if i + 1 < NB:
-                q0(i + 1)
-                mm1(i + 1)
-            if i >= 1:
-                ocopy(i - 1)
-            if i + AHEAD < NB:
-                load_w0(i + AHEAD, 1)
-            if i >= 1:
-                store(i - 1)
-            if i + AHEAD < NB:
-                load_w1(i + AHEAD)
-            if i + 1 < NB:
-                new_g1(i + 1)
-                ilv1(S, i + 1, D - S_C, D)
-                ilv1(V, i + 1, 0, D - S_C)
-                hact(i + 1)
+            new_g1(i + 1)
+            ilv1(S, i + 1, D - S_C, D)
+            ilv1(V, i + 1, 0, D - S_C)
             qh(i)
+            mm2(i)
+            if i >= 2:
+                ocopy(S, i - 2)
             if i + 2 < NB:
                 qx(i + 2)
+            if i + AHEAD < NB:
+                load_w0(i + AHEAD, 1)
+                load_w1(i + AHEAD)
+            if i >= 2:
+                store(i - 2)
 
-        b = NB - 1
+        b = last
+        otrans(b - 2)
+        hact(b)
+        new_hg(b)
+        hilv(S, b, 0, P // 2)
+        yact(b - 1)
+        q1(b)
+        hilv(V, b, P // 2, P)
+        ocopy(V, b - 2)
+        store(b - 2)
+        qh(b)
+        otrans(b - 1)
         halves = []
         for h in range(2):
             zh = psum.tile([P, 2, P], F32, name="zh", tag="z2")
             for T in range(2):
                 mm2_into(zh[:, T, :], b, 2 * h + T)
             halves.append(zh)
+        ocopy(V, b - 1)
+        store(b - 1)
         ys, os_ = [], []
         for h in range(2):
             yh = work.tile([P, 2, P], F32, name="yh", tag="y", align_bytes=64)

@@ -20,8 +20,8 @@ ALU = mybir.AluOpType
 
 FLOPS = 2 * 2 * NB * P * D * D
 
-S_M = 28
-S_C = 112
+SHARES = {0: (40, 208), 1: (40, 160), 2: (40, 144), NB - 1: (24, 32)}
+SHARE = (32, 112)
 AHEAD = 6
 RUN = 8
 
@@ -36,10 +36,9 @@ def tile_can_kernel(tc, xbytes, xscale, item, out):
         ctx.enter_context(tc.manual_schedule())
 
         raw0, raw1 = {}, {}
-        g0, g1 = {}, {}
-        c0, s0, c1, s1 = {}, {}, {}, {}
-        xs, xt, xg, xc, xsc = {}, {}, {}, {}, {}
-        z1, hp, hg, hc, hsc = {}, {}, {}, {}, {}
+        wg, wc, ws = {}, {}, {}
+        ag, ac, asc = {}, {}, {}
+        xs, xt, z1, hp = {}, {}, {}, {}
         z2, y, o, res = {}, {}, {}, {}
 
         s4 = const.tile([P, PACK], F32, name="s4")
@@ -67,12 +66,10 @@ def tile_can_kernel(tc, xbytes, xscale, item, out):
             off = layer * (W_LEN + D)
             return item[b, off:off + W_LEN].rearrange("(p j c) -> p j c", j=PACK, c=D)
 
-        def load_w0(b, pieces):
+        def load_w0(b):
             r = rawp.tile([P, PACK, D], BF16, name="raw0", tag="raw0", align_bytes=64)
             raw0[b] = r
-            step = D // pieces
-            for q in range(pieces):
-                nc.sync.dma_start(out=r[:, :, q * step:(q + 1) * step], in_=w_src(b, 0)[:, :, q * step:(q + 1) * step])
+            nc.sync.dma_start(out=r[:], in_=w_src(b, 0))
 
         def load_w1(b):
             r = rawp.tile([P, PACK, D], BF16, name="raw1", tag="raw1", align_bytes=64)
@@ -92,51 +89,51 @@ def tile_can_kernel(tc, xbytes, xscale, item, out):
             for u in range(2):
                 nc.tensor.transpose(t[:, u, :], words[:, u:D // 2:2], ident[:])
 
+        def new_weights(i):
+            wg[i] = work.tile([P, 2, D * PACK], BF16, name="wg", tag="wg", align_bytes=64)
+
+        def new_rows(i):
+            ag[i] = work.tile([P, 2, P, PACK], BF16, name="ag", tag="ag", align_bytes=64)
+
         def xcopy(b):
-            t = work.tile([P, P, PACK], BF16, name="xg", tag="xg", align_bytes=64)
-            xg[b] = t
-            nc.scalar.copy(out=t[:].rearrange("p r j -> p (r j)").bitcast(F32).rearrange("p (r u) -> p r u", u=2),
+            nc.scalar.copy(out=ag[b - 2][:, 1].rearrange("p r j -> p (r j)").bitcast(F32).rearrange("p (r u) -> p r u", u=2),
                            in_=xt[b][:].rearrange("p u r -> p r u"))
 
-        def quant(src, width, kind, codes, scales, b):
-            c = work.tile([P, width], U32, name="c_" + kind, tag="c_" + kind, align_bytes=64)
-            s = work.tile([P, width], U8, name="s_" + kind, tag="s_" + kind, align_bytes=64)
-            codes[b], scales[b] = c, s
-            nc.vector.quantize_mx(out=c[:].bitcast(FP8X4), scales=s[:], in_=src)
+        def qw(i, a, z):
+            c = work.tile([P, 2 * D], U32, name="wc", tag="wc", align_bytes=64)
+            s = work.tile([P, 2 * D], U8, name="ws", tag="ws", align_bytes=64)
+            wc[i], ws[i] = c, s
+            nc.vector.quantize_mx(out=c[:, a * D:z * D].bitcast(FP8X4), scales=s[:, a * D:z * D],
+                                  in_=wg[i][:, a:z, :].rearrange("p w k -> p (w k)"))
 
-        def qx(b):
-            quant(xg[b][:].rearrange("p r j -> p (r j)"), P, "x", xc, xsc, b)
-
-        def q0(b):
-            quant(g0[b][:].rearrange("p t m j -> p (t m j)"), D, "w0", c0, s0, b)
-
-        def q1(b):
-            quant(g1[b][:].rearrange("p c j -> p (c j)"), D, "w1", c1, s1, b)
-
-        def qh(b):
-            quant(hg[b][:].rearrange("p n j -> p (n j)"), P, "h", hc, hsc, b)
-
-        def new_g0(b):
-            g0[b] = work.tile([P, PACK, P, PACK], BF16, name="g0", tag="g0", align_bytes=64)
-
-        def new_g1(b):
-            g1[b] = work.tile([P, D, PACK], BF16, name="g1", tag="g1", align_bytes=64)
+        def qr(i, a, z):
+            c = work.tile([P, 2 * P], U32, name="ac", tag="ac", align_bytes=64)
+            s = work.tile([P, 2 * P], U8, name="asc", tag="asc", align_bytes=64)
+            ac[i], asc[i] = c, s
+            nc.vector.quantize_mx(out=c[:, a * P:z * P].bitcast(FP8X4), scales=s[:, a * P:z * P],
+                                  in_=ag[i][:, a:z].rearrange("p w r j -> p (w r j)"))
 
         def ilv0(copy, b, m0, m1):
-            copy(out=g0[b][:, :, m0:m1, :].rearrange("p t (m e) j -> p m j t e", e=2),
+            g = wg[b - 1][:, 1, :].rearrange("p (t m j) -> p t m j", t=PACK, j=PACK)
+            copy(out=g[:, :, m0:m1, :].rearrange("p t (m e) j -> p m j t e", e=2),
                  in_=raw0[b][:, :, PACK * m0:PACK * m1].rearrange("p j (m e t) -> p m j t e", e=2, t=PACK))
 
         def ilv1(copy, b, lo, hi):
-            copy(out=g1[b][:, lo:hi, :].rearrange("p (c i) j -> p c j i", i=RUN),
+            g = wg[b][:, 0, :].rearrange("p (c j) -> p c j", j=PACK)
+            copy(out=g[:, lo:hi, :].rearrange("p (c i) j -> p c j i", i=RUN),
                  in_=raw1[b][:, :, lo:hi].rearrange("p j (c i) -> p c j i", i=RUN))
+
+        def mx(dst, step, col, rstep, half):
+            lo = half * P
+            nc.tensor.matmul_mx(out=dst, lhsT=wc[step][:, col:col + P].bitcast(FP8X4), lhsT_scale=ws[step][:, col:col + P],
+                                rhs=ac[rstep][:, lo:lo + P].bitcast(FP8X4), rhs_scale=asc[rstep][:, lo:lo + P],
+                                start=True, stop=True)
 
         def mm1(b):
             t4 = psum.tile([P, PACK, P], F32, name="z1", tag="z1")
             z1[b] = t4
             for t in range(PACK):
-                nc.tensor.matmul_mx(out=t4[:, t, :], lhsT=c0[b][:, t * P:(t + 1) * P].bitcast(FP8X4),
-                                    lhsT_scale=s0[b][:, t * P:(t + 1) * P],
-                                    rhs=xc[b][:].bitcast(FP8X4), rhs_scale=xsc[b][:], start=True, stop=True)
+                mx(t4[:, t, :], b - 1, D + t * P, b - 2, 1)
 
         def hact(b):
             t4 = work.tile([P, PACK, P], BF16, name="hp", tag="hp", align_bytes=64)
@@ -144,17 +141,12 @@ def tile_can_kernel(tc, xbytes, xscale, item, out):
             for t in range(PACK):
                 nc.scalar.activation(out=t4[:, t, :], in_=z1[b][:, t, :], func=ACT.Relu, bias=bias[:, t, b:b + 1])
 
-        def new_hg(b):
-            hg[b] = work.tile([P, P, PACK], BF16, name="hg", tag="hg", align_bytes=64)
-
         def hilv(copy, b, lo, hi):
-            copy(out=hg[b][:, lo:hi, :].rearrange("p (c i) j -> p c j i", i=RUN),
+            copy(out=ag[b][:, 0, lo:hi, :].rearrange("p (c i) j -> p c j i", i=RUN),
                  in_=hp[b][:, :, lo:hi].rearrange("p j (c i) -> p c j i", i=RUN))
 
         def mm2_into(dst, b, T):
-            nc.tensor.matmul_mx(out=dst, lhsT=c1[b][:, T * P:(T + 1) * P].bitcast(FP8X4),
-                                lhsT_scale=s1[b][:, T * P:(T + 1) * P],
-                                rhs=hc[b][:].bitcast(FP8X4), rhs_scale=hsc[b][:], start=True, stop=True)
+            mx(dst, b, T * P, b, 0)
 
         def mm2(b):
             t4 = psum.tile([P, PACK, P], F32, name="z2", tag="z2")
@@ -182,15 +174,17 @@ def tile_can_kernel(tc, xbytes, xscale, item, out):
         def store(b):
             nc.sync.dma_start(out=out[b], in_=res[b][:])
 
-        load_x(0, 1)
-        load_w0(0, 2)
+        r0 = rawp.tile([P, PACK, D], BF16, name="raw0", tag="raw0", align_bytes=64)
+        raw0[0] = r0
+        nc.sync.dma_start(out=r0[:, :, 0:D // 2], in_=w_src(0, 0)[:, :, 0:D // 2])
+        load_x(0, 2)
+        nc.sync.dma_start(out=r0[:, :, D // 2:D], in_=w_src(0, 0)[:, :, D // 2:D])
         load_w1(0)
-        load_x(1, 4)
-        load_w0(1, 1)
+        load_w0(1)
+        load_x(2, NB)
         load_w1(1)
-        load_x(4, NB)
         for b in range(2, AHEAD):
-            load_w0(b, 1)
+            load_w0(b)
             load_w1(b)
 
         spread = psum.tile([P, PACK, P], F32, name="spread", tag="o")
@@ -198,89 +192,94 @@ def tile_can_kernel(tc, xbytes, xscale, item, out):
             nc.tensor.transpose(spread[:, j, :], s4[:, j:j + 1].to_broadcast([P, P]), ident[:])
         nc.scalar.copy(out=scale_all[:], in_=spread[:].rearrange("p j n -> p n j"))
 
+        V, S = nc.vector.tensor_copy, nc.scalar.copy
+
+        def share0(b):
+            m = SHARES.get(b, SHARE)[0]
+            ilv0(S, b, P - m, P)
+            ilv0(V, b, 0, P - m)
+
+        def share1(b):
+            c = SHARES.get(b, SHARE)[1]
+            ilv1(S, b, D - c, D)
+            ilv1(V, b, 0, D - c)
+
+        m = SHARES[0][0] // 2
+        new_weights(-1)
+        new_rows(-2)
+        new_rows(-1)
+        ilv0(S, 0, 0, m)
+        ilv0(V, 0, m, P // 2)
+        xprod(0)
+        ilv0(S, 0, P - m, P)
+        ilv0(V, 0, P // 2, P - m)
+        xtrans(0)
+        xcopy(0)
+        xprod(1)
+        xtrans(1)
         biases = psum.tile([P, 8, P], BF16, name="biases", tag="z2")
         for t in range(PACK):
             nc.tensor.transpose(biases[:, t, :], brow[:, 0, t:D:PACK], ident_bf[:])
         for t in range(PACK):
             nc.tensor.transpose(biases[:, PACK + t, :], brow[:, 1, t * P:(t + 1) * P], ident_bf[:])
-
-        V, S = nc.vector.tensor_copy, nc.scalar.copy
-        xprod(0)
-        xtrans(0)
-        new_g0(0)
-        ilv0(S, 0, 0, 20)
-        ilv0(V, 0, 20, 64)
-        xcopy(0)
-        ilv0(V, 0, 64, 108)
-        ilv0(S, 0, 108, 128)
-        qx(0)
-        xprod(1)
-        xtrans(1)
-        q0(0)
+        qr(-2, 1, 2)
+        qw(-1, 1, 2)
         mm1(0)
-        nc.vector.tensor_copy(out=bias[:], in_=biases[:, :, 0:NB])
         xcopy(1)
-        new_g1(0)
-        ilv1(S, 0, D - S_C, D)
-        ilv1(V, 0, 0, D - S_C)
-        qx(1)
+        new_weights(0)
+        share1(0)
+        nc.vector.tensor_copy(out=bias[:], in_=biases[:, :, 0:NB])
+        qr(-1, 1, 2)
 
         last = NB - 1
         for i in range(last):
+            share0(i + 1)
             if i + 2 < NB:
                 xprod(i + 2)
-            new_g0(i + 1)
-            ilv0(S, i + 1, P - S_M, P)
-            ilv0(V, i + 1, 0, P - S_M)
-            if i + 2 < NB:
-                xtrans(i + 2)
             if i >= 2:
                 otrans(i - 2)
+            if i + 2 < NB:
+                xtrans(i + 2)
+            new_rows(i)
             hact(i)
             if i >= 1:
                 yact(i - 1)
-            new_hg(i)
             hilv(S, i, 0, P)
-            q1(i)
-            q0(i + 1)
+            qw(i, 0, 2)
             mm1(i + 1)
             if i + 2 < NB:
                 xcopy(i + 2)
-            new_g1(i + 1)
-            ilv1(S, i + 1, D - S_C, D)
-            ilv1(V, i + 1, 0, D - S_C)
-            qh(i)
+            new_weights(i + 1)
+            share1(i + 1)
+            qr(i, 0, 2 if i + 2 < NB else 1)
             mm2(i)
             if i >= 2:
                 ocopy(S, i - 2)
-            if i + 2 < NB:
-                qx(i + 2)
             if i + AHEAD < NB:
-                load_w0(i + AHEAD, 1)
+                load_w0(i + AHEAD)
                 load_w1(i + AHEAD)
             if i >= 2:
                 store(i - 2)
 
         b = last
+        new_rows(b)
         otrans(b - 2)
         hact(b)
-        new_hg(b)
         hilv(S, b, 0, P // 2)
         yact(b - 1)
-        q1(b)
+        qw(b, 0, 1)
         hilv(V, b, P // 2, P)
-        ocopy(V, b - 2)
+        qr(b, 0, 1)
+        ocopy(S, b - 2)
         store(b - 2)
-        qh(b)
         otrans(b - 1)
+
         halves = []
         for h in range(2):
             zh = psum.tile([P, 2, P], F32, name="zh", tag="z2")
             for T in range(2):
                 mm2_into(zh[:, T, :], b, 2 * h + T)
             halves.append(zh)
-        ocopy(V, b - 1)
-        store(b - 1)
         ys, os_ = [], []
         for h in range(2):
             yh = work.tile([P, 2, P], F32, name="yh", tag="y", align_bytes=64)
@@ -292,6 +291,8 @@ def tile_can_kernel(tc, xbytes, xscale, item, out):
                     nc.vector.tensor_scalar(out=yh[:, T, :], in0=halves[h][:, T, :], scalar1=col, scalar2=0.0,
                                             op0=ALU.add, op1=ALU.max)
             ys.append(yh)
+        ocopy(V, b - 1)
+        store(b - 1)
         for h in range(2):
             oh = psum.tile([P, 2, P], F32, name="oh", tag="o")
             for T in range(2):

from contextlib import ExitStack

import concourse.mybir as mybir
from concourse.masks import make_identity

P = 128
NB, D = 16, 512
W_LEN = D * D
SAMPLE = 2 * (W_LEN + D)
PACK = 4

F32 = mybir.dt.float32
BF16 = mybir.dt.bfloat16
U32 = mybir.dt.uint32
U8 = mybir.dt.uint8
FP8 = mybir.dt.float8_e4m3fn
FP8X4 = mybir.dt.float8_e4m3fn_x4
ACT = mybir.ActivationFunctionType
ALU = mybir.AluOpType

FLOPS = 2 * 2 * NB * P * D * D

SHARES = {0: (40, 208), 1: (40, 160), 2: (40, 144), NB - 1: (24, 32)}
SHARE = (32, 112)
AHEAD = 6
RUN = 8


def tile_can_kernel(tc, xbytes, xscale, item, out):
    nc = tc.nc
    with ExitStack() as ctx:
        const = ctx.enter_context(tc.tile_pool(name="const", bufs=1))
        rawp = ctx.enter_context(tc.tile_pool(name="rawp", bufs=AHEAD))
        work = ctx.enter_context(tc.tile_pool(name="work", bufs=3))
        psum = ctx.enter_context(tc.psum_pool(name="psum", bufs=2))
        ctx.enter_context(tc.manual_schedule())

        raw0, raw1 = {}, {}
        wg, wc, ws = {}, {}, {}
        ag, ac, asc = {}, {}, {}
        xs, xt, z1, hp = {}, {}, {}, {}
        z2, y, o, res = {}, {}, {}, {}

        s4 = const.tile([P, PACK], F32, name="s4")
        brow = const.tile([P, 2, D], BF16, name="brow")
        dummy = const.tile([P, 1], F32, name="dummy")
        ident = const.tile([P, P], F32, name="ident")
        ident_bf = const.tile([P, P], BF16, name="ident_bf")
        scale_all = const.tile([P, P, PACK], F32, name="scale_all")
        bias = const.tile([P, 8, NB], F32, name="bias")
        x_bytes = const.tile([P, NB, D], U8, name="x_bytes")

        nc.scalar.dma_start(out=s4[:], in_=xscale.rearrange("a q (p j) -> p (a q j)", j=PACK))
        nc.vector.memset(dummy[:], 0.0)
        nc.vector.memset(brow[:], 0.0)
        nc.scalar.dma_start(out=brow[0:NB, 0, :], in_=item[:, W_LEN:W_LEN + D])
        nc.scalar.dma_start(out=brow[0:NB, 1, :], in_=item[:, SAMPLE - D:SAMPLE])
        nc.scalar.activation(out=dummy[:], in_=dummy[:], func=ACT.Relu)
        make_identity(nc, ident[:])
        nc.vector.tensor_copy(out=ident_bf[:], in_=ident[:])

        def load_x(b0, b1):
            nc.sync.dma_start(out=x_bytes[:, b0:b1, :], in_=xbytes[b0:b1].rearrange("b r k -> r b k"))

        def w_src(b, layer):
            off = layer * (W_LEN + D)
            return item[b, off:off + W_LEN].rearrange("(p j c) -> p j c", j=PACK, c=D)

        def load_w0(b):
            r = rawp.tile([P, PACK, D], BF16, name="raw0", tag="raw0", align_bytes=64)
            raw0[b] = r
            nc.sync.dma_start(out=r[:], in_=w_src(b, 0))

        def load_w1(b):
            r = rawp.tile([P, PACK, D], BF16, name="raw1", tag="raw1", align_bytes=64)
            raw1[b] = r
            nc.sync.dma_start(out=r[:], in_=w_src(b, 1))

        def xprod(b):
            t = work.tile([P, D], BF16, name="xs", tag="xs", align_bytes=64)
            xs[b] = t
            nc.vector.tensor_tensor(out=t[:], in0=x_bytes[:, b, :].bitcast(FP8),
                                    in1=scale_all[:].rearrange("p n j -> p (n j)"), op=ALU.mult)

        def xtrans(b):
            t = psum.tile([P, 2, P], F32, name="xt", tag="xt")
            xt[b] = t
            words = xs[b][:].bitcast(F32)
            for u in range(2):
                nc.tensor.transpose(t[:, u, :], words[:, u:D // 2:2], ident[:])

        def new_weights(i):
            wg[i] = work.tile([P, 2, D * PACK], BF16, name="wg", tag="wg", align_bytes=64)

        def new_rows(i):
            ag[i] = work.tile([P, 2, P, PACK], BF16, name="ag", tag="ag", align_bytes=64)

        def xcopy(b):
            nc.scalar.copy(out=ag[b - 2][:, 1].rearrange("p r j -> p (r j)").bitcast(F32).rearrange("p (r u) -> p r u", u=2),
                           in_=xt[b][:].rearrange("p u r -> p r u"))

        def qw(i, a, z):
            c = work.tile([P, 2 * D], U32, name="wc", tag="wc", align_bytes=64)
            s = work.tile([P, 2 * D], U8, name="ws", tag="ws", align_bytes=64)
            wc[i], ws[i] = c, s
            nc.vector.quantize_mx(out=c[:, a * D:z * D].bitcast(FP8X4), scales=s[:, a * D:z * D],
                                  in_=wg[i][:, a:z, :].rearrange("p w k -> p (w k)"))

        def qr(i, a, z):
            c = work.tile([P, 2 * P], U32, name="ac", tag="ac", align_bytes=64)
            s = work.tile([P, 2 * P], U8, name="asc", tag="asc", align_bytes=64)
            ac[i], asc[i] = c, s
            nc.vector.quantize_mx(out=c[:, a * P:z * P].bitcast(FP8X4), scales=s[:, a * P:z * P],
                                  in_=ag[i][:, a:z].rearrange("p w r j -> p (w r j)"))

        def ilv0(copy, b, m0, m1):
            g = wg[b - 1][:, 1, :].rearrange("p (t m j) -> p t m j", t=PACK, j=PACK)
            copy(out=g[:, :, m0:m1, :].rearrange("p t (m e) j -> p m j t e", e=2),
                 in_=raw0[b][:, :, PACK * m0:PACK * m1].rearrange("p j (m e t) -> p m j t e", e=2, t=PACK))

        def ilv1(copy, b, lo, hi):
            g = wg[b][:, 0, :].rearrange("p (c j) -> p c j", j=PACK)
            copy(out=g[:, lo:hi, :].rearrange("p (c i) j -> p c j i", i=RUN),
                 in_=raw1[b][:, :, lo:hi].rearrange("p j (c i) -> p c j i", i=RUN))

        def mx(dst, step, col, rstep, half):
            lo = half * P
            nc.tensor.matmul_mx(out=dst, lhsT=wc[step][:, col:col + P].bitcast(FP8X4), lhsT_scale=ws[step][:, col:col + P],
                                rhs=ac[rstep][:, lo:lo + P].bitcast(FP8X4), rhs_scale=asc[rstep][:, lo:lo + P],
                                start=True, stop=True)

        def mm1(b):
            t4 = psum.tile([P, PACK, P], F32, name="z1", tag="z1")
            z1[b] = t4
            for t in range(PACK):
                mx(t4[:, t, :], b - 1, D + t * P, b - 2, 1)

        def hact(b):
            t4 = work.tile([P, PACK, P], BF16, name="hp", tag="hp", align_bytes=64)
            hp[b] = t4
            for t in range(PACK):
                nc.scalar.activation(out=t4[:, t, :], in_=z1[b][:, t, :], func=ACT.Relu, bias=bias[:, t, b:b + 1])

        def hilv(copy, b, lo, hi):
            copy(out=ag[b][:, 0, lo:hi, :].rearrange("p (c i) j -> p c j i", i=RUN),
                 in_=hp[b][:, :, lo:hi].rearrange("p j (c i) -> p c j i", i=RUN))

        def mm2_into(dst, b, T):
            mx(dst, b, T * P, b, 0)

        def mm2(b):
            t4 = psum.tile([P, PACK, P], F32, name="z2", tag="z2")
            z2[b] = t4
            for T in range(PACK):
                mm2_into(t4[:, T, :], b, T)

        def yact(b):
            t4 = work.tile([P, PACK, P], F32, name="y", tag="y", align_bytes=64)
            y[b] = t4
            for T in range(PACK):
                nc.scalar.activation(out=t4[:, T, :], in_=z2[b][:, T, :], func=ACT.Relu, bias=bias[:, PACK + T, b:b + 1])

        def otrans(b):
            t4 = psum.tile([P, PACK, P], F32, name="o", tag="o")
            o[b] = t4
            for T in range(PACK):
                nc.tensor.transpose(t4[:, T, :], y[b][:, T, :], ident[:])

        def ocopy(copy, b):
            t = work.tile([P, D], F32, name="res", tag="res", align_bytes=64)
            res[b] = t
            copy(out=t[:], in_=o[b][:].rearrange("p t n -> p (t n)"))

        def store(b):
            nc.sync.dma_start(out=out[b], in_=res[b][:])

        r0 = rawp.tile([P, PACK, D], BF16, name="raw0", tag="raw0", align_bytes=64)
        raw0[0] = r0
        nc.sync.dma_start(out=r0[:, :, 0:D // 2], in_=w_src(0, 0)[:, :, 0:D // 2])
        load_x(0, 2)
        nc.sync.dma_start(out=r0[:, :, D // 2:D], in_=w_src(0, 0)[:, :, D // 2:D])
        load_w1(0)
        load_w0(1)
        load_x(2, NB)
        load_w1(1)
        for b in range(2, AHEAD):
            load_w0(b)
            load_w1(b)

        spread = psum.tile([P, PACK, P], F32, name="spread", tag="o")
        for j in range(PACK):
            nc.tensor.transpose(spread[:, j, :], s4[:, j:j + 1].to_broadcast([P, P]), ident[:])
        nc.scalar.copy(out=scale_all[:], in_=spread[:].rearrange("p j n -> p n j"))

        V, S = nc.vector.tensor_copy, nc.scalar.copy

        def share0(b):
            m = SHARES.get(b, SHARE)[0]
            ilv0(S, b, P - m, P)
            ilv0(V, b, 0, P - m)

        def share1(b):
            c = SHARES.get(b, SHARE)[1]
            ilv1(S, b, D - c, D)
            ilv1(V, b, 0, D - c)

        m = SHARES[0][0] // 2
        new_weights(-1)
        new_rows(-2)
        new_rows(-1)
        ilv0(S, 0, 0, m)
        ilv0(V, 0, m, P // 2)
        xprod(0)
        ilv0(S, 0, P - m, P)
        ilv0(V, 0, P // 2, P - m)
        xtrans(0)
        xcopy(0)
        xprod(1)
        xtrans(1)
        biases = psum.tile([P, 8, P], BF16, name="biases", tag="z2")
        for t in range(PACK):
            nc.tensor.transpose(biases[:, t, :], brow[:, 0, t:D:PACK], ident_bf[:])
        for t in range(PACK):
            nc.tensor.transpose(biases[:, PACK + t, :], brow[:, 1, t * P:(t + 1) * P], ident_bf[:])
        qr(-2, 1, 2)
        qw(-1, 1, 2)
        mm1(0)
        xcopy(1)
        new_weights(0)
        share1(0)
        nc.vector.tensor_copy(out=bias[:], in_=biases[:, :, 0:NB])
        qr(-1, 1, 2)

        last = NB - 1
        for i in range(last):
            share0(i + 1)
            if i + 2 < NB:
                xprod(i + 2)
            if i >= 2:
                otrans(i - 2)
            if i + 2 < NB:
                xtrans(i + 2)
            new_rows(i)
            hact(i)
            if i >= 1:
                yact(i - 1)
            hilv(S, i, 0, P)
            qw(i, 0, 2)
            mm1(i + 1)
            if i + 2 < NB:
                xcopy(i + 2)
            new_weights(i + 1)
            share1(i + 1)
            qr(i, 0, 2 if i + 2 < NB else 1)
            mm2(i)
            if i >= 2:
                ocopy(S, i - 2)
            if i + AHEAD < NB:
                load_w0(i + AHEAD)
                load_w1(i + AHEAD)
            if i >= 2:
                store(i - 2)

        b = last
        new_rows(b)
        otrans(b - 2)
        hact(b)
        hilv(S, b, 0, P // 2)
        yact(b - 1)
        qw(b, 0, 1)
        hilv(V, b, P // 2, P)
        qr(b, 0, 1)
        ocopy(S, b - 2)
        store(b - 2)
        otrans(b - 1)

        halves = []
        for h in range(2):
            zh = psum.tile([P, 2, P], F32, name="zh", tag="z2")
            for T in range(2):
                mm2_into(zh[:, T, :], b, 2 * h + T)
            halves.append(zh)
        ys, os_ = [], []
        for h in range(2):
            yh = work.tile([P, 2, P], F32, name="yh", tag="y", align_bytes=64)
            for T in range(2):
                col = bias[:, PACK + 2 * h + T, b:b + 1]
                if h == 0:
                    nc.scalar.activation(out=yh[:, T, :], in_=halves[h][:, T, :], func=ACT.Relu, bias=col)
                else:
                    nc.vector.tensor_scalar(out=yh[:, T, :], in0=halves[h][:, T, :], scalar1=col, scalar2=0.0,
                                            op0=ALU.add, op1=ALU.max)
            ys.append(yh)
        ocopy(V, b - 1)
        store(b - 1)
        for h in range(2):
            oh = psum.tile([P, 2, P], F32, name="oh", tag="o")
            for T in range(2):
                nc.tensor.transpose(oh[:, T, :], ys[h][:, T, :], ident[:])
            os_.append(oh)
        for h in range(2):
            rh = work.tile([P, 2 * P], F32, name="rh", tag="res", align_bytes=64)
            cols = slice(2 * P * h, 2 * P * (h + 1))
            if h == 0:
                nc.scalar.copy(out=rh[:], in_=os_[h][:].rearrange("p t n -> p (t n)"))
                nc.sync.dma_start(out=out[b, :, cols], in_=rh[:])
            else:
                nc.vector.tensor_copy(out=rh[:], in_=os_[h][:].rearrange("p t n -> p (t n)"))
                nc.scalar.dma_start(out=out[b, :, cols], in_=rh[:])
